import numpy as np
import ml_dtypes


def mxq(x, axis, fmt="e4m3"):
    dtype, down = {"e4m3": (ml_dtypes.float8_e4m3fn, 7), "e5m2": (ml_dtypes.float8_e5m2, 14)}[fmt]
    v = np.moveaxis(np.asarray(x, np.float32).astype(ml_dtypes.bfloat16).astype(np.float64), axis, -1)
    blocks = v.reshape(v.shape[:-1] + (-1, 32))
    amax = np.abs(blocks).max(-1, keepdims=True)
    byte = np.maximum(np.where(amax > 0, np.frexp(amax)[1] - 1 + 127, 0) - down, 1)
    scale = np.exp2(byte - 127.0)
    codes = (blocks / scale).astype(np.float32).astype(dtype).astype(np.float64)
    return np.moveaxis((codes * scale).reshape(v.shape), -1, axis)


WIDE = False


def mx_kscale(k):
    if not WIDE:
        return np.ones(k)
    levels = np.array([20, -20, 10, -10, 0])
    a = np.random.permutation(np.resize(levels, k // 512 * 4)).reshape(k // 512, 4)
    idx = np.arange(k)
    return np.exp2(a[idx // 512, idx % 128 // 32])


BF16 = ml_dtypes.bfloat16


def bf(x):
    return np.asarray(x, np.float32).astype(BF16)


def f64(x):
    return np.asarray(x).astype(np.float64)


B, P, D, R = 2048, 1024, 1024, 4


def kernel_values(x, prototypes, sigma):
    x_sq = np.sum(x * x, axis=1, keepdims=True)
    p_sq = np.sum(prototypes * prototypes, axis=1)[None]
    cross = x @ prototypes.T
    d2 = x_sq + p_sq - 2.0 * cross
    return np.exp(-d2 / (2.0 * sigma * sigma))


def setup_inputs():
    u = mx_kscale(P)
    basis = np.random.standard_normal((R, D)) / np.sqrt(D)
    x0 = bf(1.2 * np.random.standard_normal((B, R)) @ basis + 0.8 * np.random.standard_normal((B, D)) / np.sqrt(D))
    p0 = bf(1.2 * np.random.standard_normal((P, R)) @ basis + 0.8 * np.random.standard_normal((P, D)) / np.sqrt(D))
    g = bf(np.random.standard_normal((B, P)) * np.exp2(np.random.randint(-12, 1, (B, 1))) * 16.0 * u[None, :])
    kern = kernel_values(f64(x0), f64(p0), 2.0)
    return {"x": bf(f64(x0) / np.max(u)), "prototypes": bf(f64(p0) / u[:, None]), "sigma": 2,
            "kern": np.asarray(kern, np.float32), "grad_out": g}


def reference(x, prototypes, sigma, kern, grad_out):
    x, prototypes, sigma = f64(x), f64(prototypes), f64(sigma)
    w = f64(grad_out) * f64(kern)
    rs = np.sum(w, axis=1, keepdims=True)
    wp = mxq(w, 1, "e5m2") @ mxq(prototypes, 0, "e4m3")
    return (wp - x * rs) / (sigma * sigma)

@@ -1,0 +1,188 @@
+from contextlib import ExitStack
+
+import concourse.mybir as mybir
+from concourse.masks import make_identity
+
+F32 = mybir.dt.float32
+BF16 = mybir.dt.bfloat16
+U32 = mybir.dt.uint32
+U8 = mybir.dt.uint8
+E4M3_X4 = mybir.dt.float8_e4m3fn_x4
+E5M2_X4 = mybir.dt.float8_e5m2_x4
+MULT = mybir.AluOpType.mult
+ADD = mybir.AluOpType.add
+COPY = mybir.ActivationFunctionType.Copy
+
+TOKENS = 2048
+PROTOS = 1024
+FEATURES = 1024
+P = 128
+PACK = 4
+K_PASS = P * PACK
+PASSES = PROTOS // K_PASS
+N_TILE = 512
+N_TILES = FEATURES // N_TILE
+TOKEN_TILES = TOKENS // P
+CHUNK = 2
+CHUNKS = TOKEN_TILES // CHUNK
+RUN = 4
+
+FLOPS = 2 * TOKENS * PROTOS * FEATURES
+
+assert PROTOS == FEATURES
+
+
+def tile_kernel_layer_t_v_kernel(tc, x, prototypes, sigma, kern, grad_out, out):
+    nc = tc.nc
+    inv_sigma2 = 1.0 / float(sigma * sigma)
+
+    x_view = x.rearrange("(p i) d -> p i d", i=TOKEN_TILES)
+    kern_view = kern.rearrange("(p i) k -> p i k", i=TOKEN_TILES)
+    grad_view = grad_out.rearrange("(p i) k -> p i k", i=TOKEN_TILES)
+    out_view = out.rearrange("(p i) d -> p i d", i=TOKEN_TILES)
+
+    with ExitStack() as ctx:
+        resident = ctx.enter_context(tc.tile_pool(name="resident", bufs=1))
+        w_pool = ctx.enter_context(tc.tile_pool(name="w_pool", bufs=3))
+        transposed_psum = ctx.enter_context(tc.psum_pool(name="transposed_psum", bufs=4))
+        product_psum = ctx.enter_context(tc.psum_pool(name="product_psum", bufs=4))
+        ctx.enter_context(tc.manual_schedule())
+
+        identity = resident.tile([P, P], F32, name="identity")
+        make_identity(nc, identity[:])
+
+        proto_raw = [resident.tile([P, PACK, FEATURES], BF16, name="proto_raw%d" % g) for g in range(PASSES)]
+        grad_rows = [resident.tile([P, CHUNK, PROTOS], BF16, name="grad_rows%d" % c) for c in range(CHUNKS)]
+        x_rows = [resident.tile([P, CHUNK, FEATURES], BF16, name="x_rows%d" % c) for c in range(CHUNKS)]
+        f32_rows = [resident.tile([P, CHUNK, PROTOS], F32, name="f32_rows%d" % c) for c in range(CHUNKS)]
+
+        def load_w_inputs(c):
+            tiles = slice(c * CHUNK, (c + 1) * CHUNK)
+            nc.sync.dma_start(out=grad_rows[c][:], in_=grad_view[:, tiles, :])
+            nc.sync.dma_start(out=f32_rows[c][:], in_=kern_view[:, tiles, :])
+
+        def load_x(c):
+            tiles = slice(c * CHUNK, (c + 1) * CHUNK)
+            nc.sync.dma_start(out=x_rows[c][:], in_=x_view[:, tiles, :])
+
+        for g in range(PASSES):
+            rows = prototypes[g * K_PASS : (g + 1) * K_PASS, :]
+            nc.sync.dma_start(out=proto_raw[g][:], in_=rows.rearrange("(t p) n -> p t n", p=P))
+        load_w_inputs(0)
+        for c in range(1, CHUNKS):
+            load_w_inputs(c)
+            load_x(c - 1)
+        load_x(CHUNKS - 1)
+
+        proto_codes = resident.tile([P, PASSES, FEATURES], U32, align_bytes=64, name="proto_codes")
+        proto_scales = resident.tile([P, PASSES, FEATURES], U8, align_bytes=64, name="proto_scales")
+        proto_grouped = {}
+
+        def regroup_prototypes(g, h, copy):
+            grouped = resident.tile([P, N_TILE, PACK], BF16, align_bytes=64, name="proto_grouped%d%d" % (g, h))
+            proto_grouped[(g, h)] = grouped
+            copy(
+                out=grouped[:].rearrange("p (c i) t -> p c t i", i=RUN),
+                in_=proto_raw[g][:, :, h * N_TILE : (h + 1) * N_TILE].rearrange("p t (c i) -> p c t i", i=RUN),
+            )
+
+        def quantise_prototypes(g, h):
+            cols = slice(h * N_TILE, (h + 1) * N_TILE)
+            nc.vector.quantize_mx(
+                out=proto_codes[:, g, cols].bitcast(E4M3_X4),
+                scales=proto_scales[:, g, cols],
+                in_=proto_grouped[(g, h)][:].rearrange("p n t -> p (n t)"),
+            )
+
+        for g in range(PASSES):
+            regroup_prototypes(g, 0, nc.vector.tensor_copy)
+            regroup_prototypes(g, 1, nc.scalar.copy)
+            quantise_prototypes(g, 0)
+        for g in range(PASSES):
+            quantise_prototypes(g, 1)
+
+        row_sum = resident.tile([P, TOKEN_TILES], F32, name="row_sum")
+        x_factor = resident.tile([P, TOKEN_TILES], F32, name="x_factor")
+        w_grouped = {}
+        products = {}
+
+        def multiply(i):
+            c, j = divmod(i, CHUNK)
+            nc.vector.scalar_tensor_tensor(
+                out=f32_rows[c][:, j, :],
+                in0=grad_rows[c][:, j, :],
+                scalar=1.0,
+                in1=f32_rows[c][:, j, :],
+                op0=MULT,
+                op1=MULT,
+                accum_out=row_sum[:, i : i + 1],
+            )
+
+        def transpose(i):
+            c, j = divmod(i, CHUNK)
+            grouped = w_pool.tile([P, PASSES, P, PACK], BF16, align_bytes=64, name="w_grouped")
+            w_grouped[i] = grouped
+            for g in range(PASSES):
+                transposed = transposed_psum.tile([P, PACK, P], F32, name="transposed")
+                for t in range(PACK):
+                    k0 = g * K_PASS + t * P
+                    nc.tensor.transpose(transposed[:, t, :], f32_rows[c][:, j, k0 : k0 + P], identity[:])
+                nc.scalar.copy(out=grouped[:, g, :, :], in_=transposed[:].rearrange("p t r -> p r t"))
+
+        def x_term(i):
+            c, j = divmod(i, CHUNK)
+            nc.scalar.mul(out=x_factor[:, i : i + 1], in_=row_sum[:, i : i + 1], mul=-inv_sigma2)
+            nc.scalar.activation(
+                out=f32_rows[c][:, j, :], in_=x_rows[c][:, j, :], func=COPY, scale=x_factor[:, i : i + 1]
+            )
+
+        def quantise_and_matmul(i):
+            w_codes = w_pool.tile([P, PASSES * P], U32, align_bytes=64, name="w_codes")
+            w_scales = w_pool.tile([P, PASSES * P], U8, align_bytes=64, name="w_scales")
+            nc.vector.quantize_mx(
+                out=w_codes[:].bitcast(E5M2_X4),
+                scales=w_scales[:],
+                in_=w_grouped[i][:].rearrange("p g r t -> p (g r t)"),
+            )
+            products[i] = []
+            for h in range(N_TILES):
+                cols = slice(h * N_TILE, (h + 1) * N_TILE)
+                product = product_psum.tile([P, N_TILE], F32, name="product")
+                products[i].append(product)
+                for g in range(PASSES):
+                    tokens = slice(g * P, (g + 1) * P)
+                    nc.tensor.matmul_mx(
+                        out=product[:],
+                        lhsT=w_codes[:, tokens].bitcast(E5M2_X4),
+                        lhsT_scale=w_scales[:, tokens],
+                        rhs=proto_codes[:, g, cols].bitcast(E4M3_X4),
+                        rhs_scale=proto_scales[:, g, cols],
+                        start=(g == 0),
+                        stop=(g == PASSES - 1),
+                    )
+
+        def finish(i):
+            c, j = divmod(i, CHUNK)
+            for h in range(N_TILES):
+                cols = slice(h * N_TILE, (h + 1) * N_TILE)
+                nc.vector.scalar_tensor_tensor(
+                    out=f32_rows[c][:, j, cols],
+                    in0=products[i][h][:],
+                    scalar=inv_sigma2,
+                    in1=f32_rows[c][:, j, cols],
+                    op0=MULT,
+                    op1=ADD,
+                )
+            nc.sync.dma_start(out=out_view[:, i, :], in_=f32_rows[c][:, j, :])
+
+        for s in range(TOKEN_TILES + 2):
+            if s < TOKEN_TILES:
+                multiply(s)
+            if 1 <= s <= TOKEN_TILES:
+                x_term(s - 1)
+            if s < TOKEN_TILES:
+                transpose(s)
+            if 1 <= s <= TOKEN_TILES:
+                quantise_and_matmul(s - 1)
+            if s >= 2:
+                finish(s - 2)

@@ -23,8 +23,10 @@ PASSES = PROTOS // K_PASS
 N_TILE = 512
 N_TILES = FEATURES // N_TILE
 TOKEN_TILES = TOKENS // P
-CHUNK = 2
-CHUNKS = TOKEN_TILES // CHUNK
+F32_TILES = 2
+BF16_TILES = 4
+F32_CHUNKS = TOKEN_TILES // F32_TILES
+BF16_CHUNKS = TOKEN_TILES // BF16_TILES
 RUN = 4
 
 FLOPS = 2 * TOKENS * PROTOS * FEATURES
@@ -52,27 +54,24 @@ def tile_kernel_layer_t_v_kernel(tc, x, prototypes, sigma, kern, grad_out, out):
         make_identity(nc, identity[:])
 
         proto_raw = [resident.tile([P, PACK, FEATURES], BF16, name="proto_raw%d" % g) for g in range(PASSES)]
-        grad_rows = [resident.tile([P, CHUNK, PROTOS], BF16, name="grad_rows%d" % c) for c in range(CHUNKS)]
-        x_rows = [resident.tile([P, CHUNK, FEATURES], BF16, name="x_rows%d" % c) for c in range(CHUNKS)]
-        f32_rows = [resident.tile([P, CHUNK, PROTOS], F32, name="f32_rows%d" % c) for c in range(CHUNKS)]
+        grad_rows = [resident.tile([P, BF16_TILES, PROTOS], BF16, name="grad_rows%d" % b) for b in range(BF16_CHUNKS)]
+        x_rows = [resident.tile([P, BF16_TILES, FEATURES], BF16, name="x_rows%d" % b) for b in range(BF16_CHUNKS)]
+        f32_rows = [resident.tile([P, F32_TILES, PROTOS], F32, name="f32_rows%d" % c) for c in range(F32_CHUNKS)]
 
-        def load_w_inputs(c):
-            tiles = slice(c * CHUNK, (c + 1) * CHUNK)
-            nc.sync.dma_start(out=grad_rows[c][:], in_=grad_view[:, tiles, :])
-            nc.sync.dma_start(out=f32_rows[c][:], in_=kern_view[:, tiles, :])
+        def load_bf16(rows, view, b):
+            nc.sync.dma_start(out=rows[b][:], in_=view[:, b * BF16_TILES : (b + 1) * BF16_TILES, :])
 
-        def load_x(c):
-            tiles = slice(c * CHUNK, (c + 1) * CHUNK)
-            nc.sync.dma_start(out=x_rows[c][:], in_=x_view[:, tiles, :])
+        def load_kern(c):
+            nc.sync.dma_start(out=f32_rows[c][:], in_=kern_view[:, c * F32_TILES : (c + 1) * F32_TILES, :])
 
         for g in range(PASSES):
             rows = prototypes[g * K_PASS : (g + 1) * K_PASS, :]
             nc.sync.dma_start(out=proto_raw[g][:], in_=rows.rearrange("(t p) n -> p t n", p=P))
-        load_w_inputs(0)
-        for c in range(1, CHUNKS):
-            load_w_inputs(c)
-            load_x(c - 1)
-        load_x(CHUNKS - 1)
+        for b in range(BF16_CHUNKS):
+            load_bf16(grad_rows, grad_view, b)
+            load_kern(2 * b)
+            load_bf16(x_rows, x_view, b)
+            load_kern(2 * b + 1)
 
         proto_codes = resident.tile([P, PASSES, FEATURES], U32, align_bytes=64, name="proto_codes")
         proto_scales = resident.tile([P, PASSES, FEATURES], U8, align_bytes=64, name="proto_scales")
@@ -107,10 +106,10 @@ def tile_kernel_layer_t_v_kernel(tc, x, prototypes, sigma, kern, grad_out, out):
         products = {}
 
         def multiply(i):
-            c, j = divmod(i, CHUNK)
+            c, j = divmod(i, F32_TILES)
             nc.vector.scalar_tensor_tensor(
                 out=f32_rows[c][:, j, :],
-                in0=grad_rows[c][:, j, :],
+                in0=grad_rows[i // BF16_TILES][:, i % BF16_TILES, :],
                 scalar=1.0,
                 in1=f32_rows[c][:, j, :],
                 op0=MULT,
@@ -119,7 +118,7 @@ def tile_kernel_layer_t_v_kernel(tc, x, prototypes, sigma, kern, grad_out, out):
             )
 
         def transpose(i):
-            c, j = divmod(i, CHUNK)
+            c, j = divmod(i, F32_TILES)
             grouped = w_pool.tile([P, PASSES, P, PACK], BF16, align_bytes=64, name="w_grouped")
             w_grouped[i] = grouped
             for g in range(PASSES):
@@ -130,10 +129,13 @@ def tile_kernel_layer_t_v_kernel(tc, x, prototypes, sigma, kern, grad_out, out):
                 nc.scalar.copy(out=grouped[:, g, :, :], in_=transposed[:].rearrange("p t r -> p r t"))
 
         def x_term(i):
-            c, j = divmod(i, CHUNK)
+            c, j = divmod(i, F32_TILES)
             nc.scalar.mul(out=x_factor[:, i : i + 1], in_=row_sum[:, i : i + 1], mul=-inv_sigma2)
             nc.scalar.activation(
-                out=f32_rows[c][:, j, :], in_=x_rows[c][:, j, :], func=COPY, scale=x_factor[:, i : i + 1]
+                out=f32_rows[c][:, j, :],
+                in_=x_rows[i // BF16_TILES][:, i % BF16_TILES, :],
+                func=COPY,
+                scale=x_factor[:, i : i + 1],
             )
 
         def quantise_and_matmul(i):
@@ -162,7 +164,7 @@ def tile_kernel_layer_t_v_kernel(tc, x, prototypes, sigma, kern, grad_out, out):
                     )
 
         def finish(i):
-            c, j = divmod(i, CHUNK)
+            c, j = divmod(i, F32_TILES)
             for h in range(N_TILES):
                 cols = slice(h * N_TILE, (h + 1) * N_TILE)
                 nc.vector.scalar_tensor_tensor(
@@ -173,7 +175,10 @@ def tile_kernel_layer_t_v_kernel(tc, x, prototypes, sigma, kern, grad_out, out):
                     op0=MULT,
                     op1=ADD,
                 )
-            nc.sync.dma_start(out=out_view[:, i, :], in_=f32_rows[c][:, j, :])
+            if c == F32_CHUNKS - 1:
+                nc.sync.dma_start(out=out_view[:, i, :], in_=f32_rows[c][:, j, :])
+            elif j == F32_TILES - 1:
+                nc.sync.dma_start(out=out_view[:, c * F32_TILES : (c + 1) * F32_TILES, :], in_=f32_rows[c][:])
 
         for s in range(TOKEN_TILES + 2):
             if s < TOKEN_TILES:

@@ -66,7 +66,7 @@ def tile_kernel_layer_t_v_kernel(tc, x, prototypes, sigma, kern, grad_out, out):
 
         for g in range(PASSES):
             rows = prototypes[g * K_PASS : (g + 1) * K_PASS, :]
-            nc.sync.dma_start(out=proto_raw[g][:], in_=rows.rearrange("(t p) n -> p t n", p=P))
+            nc.sync.dma_start(out=proto_raw[g][:], in_=rows.rearrange("(p t) n -> p t n", t=PACK))
         for b in range(BF16_CHUNKS):
             load_bf16(grad_rows, grad_view, b)
             load_kern(2 * b)
@@ -119,13 +119,13 @@ def tile_kernel_layer_t_v_kernel(tc, x, prototypes, sigma, kern, grad_out, out):
 
         def transpose(i):
             c, j = divmod(i, F32_TILES)
+            w_by_value = f32_rows[c][:, j, :].rearrange("r (g p t) -> r g t p", g=PASSES, t=PACK)
             grouped = w_pool.tile([P, PASSES, P, PACK], BF16, align_bytes=64, name="w_grouped")
             w_grouped[i] = grouped
             for g in range(PASSES):
                 transposed = transposed_psum.tile([P, PACK, P], F32, name="transposed")
                 for t in range(PACK):
-                    k0 = g * K_PASS + t * P
-                    nc.tensor.transpose(transposed[:, t, :], f32_rows[c][:, j, k0 : k0 + P], identity[:])
+                    nc.tensor.transpose(transposed[:, t, :], w_by_value[:, g, t, :], identity[:])
                 nc.scalar.copy(out=grouped[:, g, :, :], in_=transposed[:].rearrange("p t r -> p r t"))
 
         def x_term(i):

@@ -18,6 +18,7 @@ PROTOS = 1024
 FEATURES = 1024
 P = 128
 PACK = 4
+HALVES = 2
 K_PASS = P * PACK
 PASSES = PROTOS // K_PASS
 N_TILE = 512
@@ -102,13 +103,15 @@ def tile_kernel_layer_t_v_kernel(tc, x, prototypes, sigma, kern, grad_out, out):
 
         row_sum = resident.tile([P, TOKEN_TILES], F32, name="row_sum")
         x_factor = resident.tile([P, TOKEN_TILES], F32, name="x_factor")
+        w_rows = {}
         w_grouped = {}
         products = {}
 
         def multiply(i):
             c, j = divmod(i, F32_TILES)
+            w_rows[i] = w_pool.tile([P, PROTOS], BF16, align_bytes=64, name="w_rows")
             nc.vector.scalar_tensor_tensor(
-                out=f32_rows[c][:, j, :],
+                out=w_rows[i][:],
                 in0=grad_rows[i // BF16_TILES][:, i % BF16_TILES, :],
                 scalar=1.0,
                 in1=f32_rows[c][:, j, :],
@@ -118,15 +121,14 @@ def tile_kernel_layer_t_v_kernel(tc, x, prototypes, sigma, kern, grad_out, out):
             )
 
         def transpose(i):
-            c, j = divmod(i, F32_TILES)
-            w_by_value = f32_rows[c][:, j, :].rearrange("r (g p t) -> r g t p", g=PASSES, t=PACK)
+            words = w_rows[i][:].bitcast(F32).rearrange("r (g p u) -> r g u p", g=PASSES, u=HALVES)
             grouped = w_pool.tile([P, PASSES, P, PACK], BF16, align_bytes=64, name="w_grouped")
             w_grouped[i] = grouped
+            transposed = transposed_psum.tile([P, PASSES, HALVES, P], F32, name="transposed")
             for g in range(PASSES):
-                transposed = transposed_psum.tile([P, PACK, P], F32, name="transposed")
-                for t in range(PACK):
-                    nc.tensor.transpose(transposed[:, t, :], w_by_value[:, g, t, :], identity[:])
-                nc.scalar.copy(out=grouped[:, g, :, :], in_=transposed[:].rearrange("p t r -> p r t"))
+                for u in range(HALVES):
+                    nc.tensor.transpose(transposed[:, g, u, :], words[:, g, u, :], identity[:])
+            nc.scalar.copy(out=grouped[:].bitcast(F32), in_=transposed[:].rearrange("p g u r -> p g r u"))
 
         def x_term(i):
             c, j = divmod(i, F32_TILES)

@@ -24,10 +24,9 @@ PASSES = PROTOS // K_PASS
 N_TILE = 512
 N_TILES = FEATURES // N_TILE
 TOKEN_TILES = TOKENS // P
-F32_TILES = 2
-BF16_TILES = 4
-F32_CHUNKS = TOKEN_TILES // F32_TILES
-BF16_CHUNKS = TOKEN_TILES // BF16_TILES
+LOAD_GROUPS = (4, 4, 8)
+STORE_GROUPS = (8, 4, 2, 1, 1)
+assert sum(LOAD_GROUPS) == TOKEN_TILES and sum(STORE_GROUPS) == TOKEN_TILES
 RUN = 4
 
 FLOPS = 2 * TOKENS * PROTOS * FEATURES
@@ -55,24 +54,24 @@ def tile_kernel_layer_t_v_kernel(tc, x, prototypes, sigma, kern, grad_out, out):
         make_identity(nc, identity[:])
 
         proto_raw = [resident.tile([P, PACK, FEATURES], BF16, name="proto_raw%d" % g) for g in range(PASSES)]
-        grad_rows = [resident.tile([P, BF16_TILES, PROTOS], BF16, name="grad_rows%d" % b) for b in range(BF16_CHUNKS)]
-        x_rows = [resident.tile([P, BF16_TILES, FEATURES], BF16, name="x_rows%d" % b) for b in range(BF16_CHUNKS)]
-        f32_rows = [resident.tile([P, F32_TILES, PROTOS], F32, name="f32_rows%d" % c) for c in range(F32_CHUNKS)]
+        grad_rows = resident.tile([P, TOKEN_TILES, PROTOS], BF16, name="grad_rows")
+        x_rows = resident.tile([P, TOKEN_TILES, FEATURES], BF16, name="x_rows")
+        f32_rows = resident.tile([P, TOKEN_TILES, PROTOS], F32, name="f32_rows")
 
-        def load_bf16(rows, view, b):
-            nc.sync.dma_start(out=rows[b][:], in_=view[:, b * BF16_TILES : (b + 1) * BF16_TILES, :])
-
-        def load_kern(c):
-            nc.sync.dma_start(out=f32_rows[c][:], in_=kern_view[:, c * F32_TILES : (c + 1) * F32_TILES, :])
+        def load(rows, view, first, count):
+            nc.sync.dma_start(out=rows[:, first : first + count, :], in_=view[:, first : first + count, :])
 
         for g in range(PASSES):
             rows = prototypes[g * K_PASS : (g + 1) * K_PASS, :]
             nc.sync.dma_start(out=proto_raw[g][:], in_=rows.rearrange("(p t) n -> p t n", t=PACK))
-        for b in range(BF16_CHUNKS):
-            load_bf16(grad_rows, grad_view, b)
-            load_kern(2 * b)
-            load_bf16(x_rows, x_view, b)
-            load_kern(2 * b + 1)
+        first = 0
+        for count in LOAD_GROUPS:
+            half = count // 2
+            load(grad_rows, grad_view, first, count)
+            load(f32_rows, kern_view, first, half)
+            load(x_rows, x_view, first, count)
+            load(f32_rows, kern_view, first + half, half)
+            first += count
 
         proto_codes = resident.tile([P, PASSES, FEATURES], U32, align_bytes=64, name="proto_codes")
         proto_scales = resident.tile([P, PASSES, FEATURES], U8, align_bytes=64, name="proto_scales")
@@ -103,18 +102,22 @@ def tile_kernel_layer_t_v_kernel(tc, x, prototypes, sigma, kern, grad_out, out):
 
         row_sum = resident.tile([P, TOKEN_TILES], F32, name="row_sum")
         x_factor = resident.tile([P, TOKEN_TILES], F32, name="x_factor")
+        store_first = {}
+        first = 0
+        for count in STORE_GROUPS:
+            store_first[first + count - 1] = first
+            first += count
         w_rows = {}
         w_grouped = {}
         products = {}
 
         def multiply(i):
-            c, j = divmod(i, F32_TILES)
             w_rows[i] = w_pool.tile([P, PROTOS], BF16, align_bytes=64, name="w_rows")
             nc.vector.scalar_tensor_tensor(
                 out=w_rows[i][:],
-                in0=grad_rows[i // BF16_TILES][:, i % BF16_TILES, :],
+                in0=grad_rows[:, i, :],
                 scalar=1.0,
-                in1=f32_rows[c][:, j, :],
+                in1=f32_rows[:, i, :],
                 op0=MULT,
                 op1=MULT,
                 accum_out=row_sum[:, i : i + 1],
@@ -131,11 +134,10 @@ def tile_kernel_layer_t_v_kernel(tc, x, prototypes, sigma, kern, grad_out, out):
             nc.scalar.copy(out=grouped[:].bitcast(F32), in_=transposed[:].rearrange("p g u r -> p g r u"))
 
         def x_term(i):
-            c, j = divmod(i, F32_TILES)
             nc.scalar.mul(out=x_factor[:, i : i + 1], in_=row_sum[:, i : i + 1], mul=-inv_sigma2)
             nc.scalar.activation(
-                out=f32_rows[c][:, j, :],
-                in_=x_rows[i // BF16_TILES][:, i % BF16_TILES, :],
+                out=f32_rows[:, i, :],
+                in_=x_rows[:, i, :],
                 func=COPY,
                 scale=x_factor[:, i : i + 1],
             )
@@ -166,21 +168,19 @@ def tile_kernel_layer_t_v_kernel(tc, x, prototypes, sigma, kern, grad_out, out):
                     )
 
         def finish(i):
-            c, j = divmod(i, F32_TILES)
             for h in range(N_TILES):
                 cols = slice(h * N_TILE, (h + 1) * N_TILE)
                 nc.vector.scalar_tensor_tensor(
-                    out=f32_rows[c][:, j, cols],
+                    out=f32_rows[:, i, cols],
                     in0=products[i][h][:],
                     scalar=inv_sigma2,
-                    in1=f32_rows[c][:, j, cols],
+                    in1=f32_rows[:, i, cols],
                     op0=MULT,
                     op1=ADD,
                 )
-            if c == F32_CHUNKS - 1:
-                nc.sync.dma_start(out=out_view[:, i, :], in_=f32_rows[c][:, j, :])
-            elif j == F32_TILES - 1:
-                nc.sync.dma_start(out=out_view[:, c * F32_TILES : (c + 1) * F32_TILES, :], in_=f32_rows[c][:])
+            if i in store_first:
+                group = slice(store_first[i], i + 1)
+                nc.sync.dma_start(out=out_view[:, group, :], in_=f32_rows[:, group, :])
 
         for s in range(TOKEN_TILES + 2):
             if s < TOKEN_TILES:

@@ -24,9 +24,9 @@ PASSES = PROTOS // K_PASS
 N_TILE = 512
 N_TILES = FEATURES // N_TILE
 TOKEN_TILES = TOKENS // P
-LOAD_GROUPS = (4, 4, 8)
+LOAD_GROUPS = ((4, 2), (4, 2), (4, 4), (4, 4))
 STORE_GROUPS = (8, 4, 2, 1, 1)
-assert sum(LOAD_GROUPS) == TOKEN_TILES and sum(STORE_GROUPS) == TOKEN_TILES
+assert sum(count for count, kern_count in LOAD_GROUPS) == TOKEN_TILES and sum(STORE_GROUPS) == TOKEN_TILES
 RUN = 4
 
 FLOPS = 2 * TOKENS * PROTOS * FEATURES
@@ -65,12 +65,12 @@ def tile_kernel_layer_t_v_kernel(tc, x, prototypes, sigma, kern, grad_out, out):
             rows = prototypes[g * K_PASS : (g + 1) * K_PASS, :]
             nc.sync.dma_start(out=proto_raw[g][:], in_=rows.rearrange("(p t) n -> p t n", t=PACK))
         first = 0
-        for count in LOAD_GROUPS:
-            half = count // 2
+        for count, kern_count in LOAD_GROUPS:
             load(grad_rows, grad_view, first, count)
-            load(f32_rows, kern_view, first, half)
+            load(f32_rows, kern_view, first, kern_count)
             load(x_rows, x_view, first, count)
-            load(f32_rows, kern_view, first + half, half)
+            for kern_first in range(first + kern_count, first + count, kern_count):
+                load(f32_rows, kern_view, kern_first, kern_count)
             first += count
 
         proto_codes = resident.tile([P, PASSES, FEATURES], U32, align_bytes=64, name="proto_codes")

@@ -27,6 +27,7 @@ TOKEN_TILES = TOKENS // P
 LOAD_GROUPS = ((4, 2), (4, 2), (4, 4), (4, 4))
 STORE_GROUPS = (8, 4, 2, 1, 1)
 assert sum(count for count, kern_count in LOAD_GROUPS) == TOKEN_TILES and sum(STORE_GROUPS) == TOKEN_TILES
+DMA_ALIGN = 256
 RUN = 4
 
 FLOPS = 2 * TOKENS * PROTOS * FEATURES
@@ -53,10 +54,12 @@ def tile_kernel_layer_t_v_kernel(tc, x, prototypes, sigma, kern, grad_out, out):
         identity = resident.tile([P, P], F32, name="identity")
         make_identity(nc, identity[:])
 
-        proto_raw = [resident.tile([P, PACK, FEATURES], BF16, name="proto_raw%d" % g) for g in range(PASSES)]
-        grad_rows = resident.tile([P, TOKEN_TILES, PROTOS], BF16, name="grad_rows")
-        x_rows = resident.tile([P, TOKEN_TILES, FEATURES], BF16, name="x_rows")
-        f32_rows = resident.tile([P, TOKEN_TILES, PROTOS], F32, name="f32_rows")
+        proto_raw = [
+            resident.tile([P, PACK, FEATURES], BF16, align_bytes=DMA_ALIGN, name="proto_raw%d" % g) for g in range(PASSES)
+        ]
+        grad_rows = resident.tile([P, TOKEN_TILES, PROTOS], BF16, align_bytes=DMA_ALIGN, name="grad_rows")
+        x_rows = resident.tile([P, TOKEN_TILES, FEATURES], BF16, align_bytes=DMA_ALIGN, name="x_rows")
+        f32_rows = resident.tile([P, TOKEN_TILES, PROTOS], F32, align_bytes=DMA_ALIGN, name="f32_rows")
 
         def load(rows, view, first, count):
             nc.sync.dma_start(out=rows[:, first : first + count, :], in_=view[:, first : first + count, :])

@@ -27,7 +27,7 @@ TOKEN_TILES = TOKENS // P
 LOAD_GROUPS = ((4, 2), (4, 2), (4, 4), (4, 4))
 STORE_GROUPS = (8, 4, 2, 1, 1)
 assert sum(count for count, kern_count in LOAD_GROUPS) == TOKEN_TILES and sum(STORE_GROUPS) == TOKEN_TILES
-DMA_ALIGN = 256
+DMA_ALIGN = 4096
 RUN = 4
 
 FLOPS = 2 * TOKENS * PROTOS * FEATURES

from contextlib import ExitStack

import concourse.mybir as mybir
from concourse.masks import make_identity

F32 = mybir.dt.float32
BF16 = mybir.dt.bfloat16
U32 = mybir.dt.uint32
U8 = mybir.dt.uint8
E4M3_X4 = mybir.dt.float8_e4m3fn_x4
E5M2_X4 = mybir.dt.float8_e5m2_x4
MULT = mybir.AluOpType.mult
ADD = mybir.AluOpType.add
COPY = mybir.ActivationFunctionType.Copy

TOKENS = 2048
PROTOS = 1024
FEATURES = 1024
P = 128
PACK = 4
HALVES = 2
K_PASS = P * PACK
PASSES = PROTOS // K_PASS
N_TILE = 512
N_TILES = FEATURES // N_TILE
TOKEN_TILES = TOKENS // P
LOAD_GROUPS = ((4, 2), (4, 2), (4, 4), (4, 4))
STORE_GROUPS = (8, 4, 2, 1, 1)
assert sum(count for count, kern_count in LOAD_GROUPS) == TOKEN_TILES and sum(STORE_GROUPS) == TOKEN_TILES
DMA_ALIGN = 4096
RUN = 4

FLOPS = 2 * TOKENS * PROTOS * FEATURES

assert PROTOS == FEATURES


def tile_kernel_layer_t_v_kernel(tc, x, prototypes, sigma, kern, grad_out, out):
    nc = tc.nc
    inv_sigma2 = 1.0 / float(sigma * sigma)

    x_view = x.rearrange("(p i) d -> p i d", i=TOKEN_TILES)
    kern_view = kern.rearrange("(p i) k -> p i k", i=TOKEN_TILES)
    grad_view = grad_out.rearrange("(p i) k -> p i k", i=TOKEN_TILES)
    out_view = out.rearrange("(p i) d -> p i d", i=TOKEN_TILES)

    with ExitStack() as ctx:
        resident = ctx.enter_context(tc.tile_pool(name="resident", bufs=1))
        w_pool = ctx.enter_context(tc.tile_pool(name="w_pool", bufs=3))
        transposed_psum = ctx.enter_context(tc.psum_pool(name="transposed_psum", bufs=4))
        product_psum = ctx.enter_context(tc.psum_pool(name="product_psum", bufs=4))
        ctx.enter_context(tc.manual_schedule())

        identity = resident.tile([P, P], F32, name="identity")
        make_identity(nc, identity[:])

        proto_raw = [
            resident.tile([P, PACK, FEATURES], BF16, align_bytes=DMA_ALIGN, name="proto_raw%d" % g) for g in range(PASSES)
        ]
        grad_rows = resident.tile([P, TOKEN_TILES, PROTOS], BF16, align_bytes=DMA_ALIGN, name="grad_rows")
        x_rows = resident.tile([P, TOKEN_TILES, FEATURES], BF16, align_bytes=DMA_ALIGN, name="x_rows")
        f32_rows = resident.tile([P, TOKEN_TILES, PROTOS], F32, align_bytes=DMA_ALIGN, name="f32_rows")

        def load(rows, view, first, count):
            nc.sync.dma_start(out=rows[:, first : first + count, :], in_=view[:, first : first + count, :])

        for g in range(PASSES):
            rows = prototypes[g * K_PASS : (g + 1) * K_PASS, :]
            nc.sync.dma_start(out=proto_raw[g][:], in_=rows.rearrange("(p t) n -> p t n", t=PACK))
        first = 0
        for count, kern_count in LOAD_GROUPS:
            load(grad_rows, grad_view, first, count)
            load(f32_rows, kern_view, first, kern_count)
            load(x_rows, x_view, first, count)
            for kern_first in range(first + kern_count, first + count, kern_count):
                load(f32_rows, kern_view, kern_first, kern_count)
            first += count

        proto_codes = resident.tile([P, PASSES, FEATURES], U32, align_bytes=64, name="proto_codes")
        proto_scales = resident.tile([P, PASSES, FEATURES], U8, align_bytes=64, name="proto_scales")
        proto_grouped = {}

        def regroup_prototypes(g, h, copy):
            grouped = resident.tile([P, N_TILE, PACK], BF16, align_bytes=64, name="proto_grouped%d%d" % (g, h))
            proto_grouped[(g, h)] = grouped
            copy(
                out=grouped[:].rearrange("p (c i) t -> p c t i", i=RUN),
                in_=proto_raw[g][:, :, h * N_TILE : (h + 1) * N_TILE].rearrange("p t (c i) -> p c t i", i=RUN),
            )

        def quantise_prototypes(g, h):
            cols = slice(h * N_TILE, (h + 1) * N_TILE)
            nc.vector.quantize_mx(
                out=proto_codes[:, g, cols].bitcast(E4M3_X4),
                scales=proto_scales[:, g, cols],
                in_=proto_grouped[(g, h)][:].rearrange("p n t -> p (n t)"),
            )

        for g in range(PASSES):
            regroup_prototypes(g, 0, nc.vector.tensor_copy)
            regroup_prototypes(g, 1, nc.scalar.copy)
            quantise_prototypes(g, 0)
        for g in range(PASSES):
            quantise_prototypes(g, 1)

        row_sum = resident.tile([P, TOKEN_TILES], F32, name="row_sum")
        x_factor = resident.tile([P, TOKEN_TILES], F32, name="x_factor")
        store_first = {}
        first = 0
        for count in STORE_GROUPS:
            store_first[first + count - 1] = first
            first += count
        w_rows = {}
        w_grouped = {}
        products = {}

        def multiply(i):
            w_rows[i] = w_pool.tile([P, PROTOS], BF16, align_bytes=64, name="w_rows")
            nc.vector.scalar_tensor_tensor(
                out=w_rows[i][:],
                in0=grad_rows[:, i, :],
                scalar=1.0,
                in1=f32_rows[:, i, :],
                op0=MULT,
                op1=MULT,
                accum_out=row_sum[:, i : i + 1],
            )

        def transpose(i):
            words = w_rows[i][:].bitcast(F32).rearrange("r (g p u) -> r g u p", g=PASSES, u=HALVES)
            grouped = w_pool.tile([P, PASSES, P, PACK], BF16, align_bytes=64, name="w_grouped")
            w_grouped[i] = grouped
            transposed = transposed_psum.tile([P, PASSES, HALVES, P], F32, name="transposed")
            for g in range(PASSES):
                for u in range(HALVES):
                    nc.tensor.transpose(transposed[:, g, u, :], words[:, g, u, :], identity[:])
            nc.scalar.copy(out=grouped[:].bitcast(F32), in_=transposed[:].rearrange("p g u r -> p g r u"))

        def x_term(i):
            nc.scalar.mul(out=x_factor[:, i : i + 1], in_=row_sum[:, i : i + 1], mul=-inv_sigma2)
            nc.scalar.activation(
                out=f32_rows[:, i, :],
                in_=x_rows[:, i, :],
                func=COPY,
                scale=x_factor[:, i : i + 1],
            )

        def quantise_and_matmul(i):
            w_codes = w_pool.tile([P, PASSES * P], U32, align_bytes=64, name="w_codes")
            w_scales = w_pool.tile([P, PASSES * P], U8, align_bytes=64, name="w_scales")
            nc.vector.quantize_mx(
                out=w_codes[:].bitcast(E5M2_X4),
                scales=w_scales[:],
                in_=w_grouped[i][:].rearrange("p g r t -> p (g r t)"),
            )
            products[i] = []
            for h in range(N_TILES):
                cols = slice(h * N_TILE, (h + 1) * N_TILE)
                product = product_psum.tile([P, N_TILE], F32, name="product")
                products[i].append(product)
                for g in range(PASSES):
                    tokens = slice(g * P, (g + 1) * P)
                    nc.tensor.matmul_mx(
                        out=product[:],
                        lhsT=w_codes[:, tokens].bitcast(E5M2_X4),
                        lhsT_scale=w_scales[:, tokens],
                        rhs=proto_codes[:, g, cols].bitcast(E4M3_X4),
                        rhs_scale=proto_scales[:, g, cols],
                        start=(g == 0),
                        stop=(g == PASSES - 1),
                    )

        def finish(i):
            for h in range(N_TILES):
                cols = slice(h * N_TILE, (h + 1) * N_TILE)
                nc.vector.scalar_tensor_tensor(
                    out=f32_rows[:, i, cols],
                    in0=products[i][h][:],
                    scalar=inv_sigma2,
                    in1=f32_rows[:, i, cols],
                    op0=MULT,
                    op1=ADD,
                )
            if i in store_first:
                group = slice(store_first[i], i + 1)
                nc.sync.dma_start(out=out_view[:, group, :], in_=f32_rows[:, group, :])

        for s in range(TOKEN_TILES + 2):
            if s < TOKEN_TILES:
                multiply(s)
            if 1 <= s <= TOKEN_TILES:
                x_term(s - 1)
            if s < TOKEN_TILES:
                transpose(s)
            if 1 <= s <= TOKEN_TILES:
                quantise_and_matmul(s - 1)
            if s >= 2:
                finish(s - 2)
